import numpy as np
import ml_dtypes


def mxq(x, axis, fmt="e4m3"):
    dtype, down = {"e4m3": (ml_dtypes.float8_e4m3fn, 7), "e5m2": (ml_dtypes.float8_e5m2, 14)}[fmt]
    v = np.moveaxis(np.asarray(x, np.float32).astype(ml_dtypes.bfloat16).astype(np.float64), axis, -1)
    blocks = v.reshape(v.shape[:-1] + (-1, 32))
    amax = np.abs(blocks).max(-1, keepdims=True)
    byte = np.maximum(np.where(amax > 0, np.frexp(amax)[1] - 1 + 127, 0) - down, 1)
    scale = np.exp2(byte - 127.0)
    codes = (blocks / scale).astype(np.float32).astype(dtype).astype(np.float64)
    return np.moveaxis((codes * scale).reshape(v.shape), -1, axis)


WIDE = False


def mx_kscale(k):
    if not WIDE:
        return np.ones(k)
    levels = np.array([10, -10, 5, -5, 0])
    a = np.random.permutation(np.resize(levels, k // 512 * 4)).reshape(k // 512, 4)
    idx = np.arange(k)
    return np.exp2(a[idx // 512, idx % 128 // 32])


BF16 = ml_dtypes.bfloat16


def bf(x):
    return np.asarray(x, np.float32).astype(BF16)


def f64(x):
    return np.asarray(x).astype(np.float64)


B, U, I, H = 256, 16, 512, 128


def sigmoid(v):
    return 1.0 / (1.0 + np.exp(-v))


def setup_inputs():
    s = mx_kscale(I)
    return {"inputs": bf(np.random.standard_normal((B, U, I)) * s),
            "hidden": bf(np.random.standard_normal((B, U, H))),
            "w_ih": bf(np.random.standard_normal((U, 3 * H, I)) / np.sqrt(I) / s),
            "w_hh": bf(np.random.standard_normal((U, 3 * H, H)) / np.sqrt(H)),
            "b_ih": bf(np.random.standard_normal((U, 3 * H)) * 0.3),
            "b_hh": bf(np.random.standard_normal((U, 3 * H)) * 0.3)}


def reference(inputs, hidden, w_ih, w_hh, b_ih, b_hh):
    h = f64(hidden)
    gx = (mxq(f64(inputs), 2, "e4m3").transpose(1, 0, 2) @ mxq(f64(w_ih), 2, "e4m3").transpose(0, 2, 1)).transpose(1, 0, 2) + f64(b_ih)
    gh = (h.transpose(1, 0, 2) @ f64(w_hh).transpose(0, 2, 1)).transpose(1, 0, 2) + f64(b_hh)
    xr, xz, xn = gx[..., :H], gx[..., H:2 * H], gx[..., 2 * H:]
    hr, hz, hn = gh[..., :H], gh[..., H:2 * H], gh[..., 2 * H:]
    r = sigmoid(xr + hr)
    z = sigmoid(xz + hz)
    n = np.tanh(xn + r * hn)
    return (1.0 - z) * n + z * h

@@ -1,0 +1,232 @@
+from contextlib import ExitStack
+
+import concourse.bass as bass
+import concourse.masks as masks
+import concourse.mybir as mybir
+import concourse.tile as tile
+
+F32 = mybir.dt.float32
+BF16 = mybir.dt.bfloat16
+U32 = mybir.dt.uint32
+U8 = mybir.dt.uint8
+FP8X4 = mybir.dt.float8_e4m3fn_x4
+ACT = mybir.ActivationFunctionType
+ALU = mybir.AluOpType
+
+P = 128
+B, U, I, H = 256, 16, 512, 128
+NPAIR = U // 2
+FLOPS = 2 * B * U * 3 * H * (I + H)
+
+
+def tile_grouptorchgru_kernel(tc, inputs, hidden, w_ih, w_hh, b_ih, b_hh, out):
+    nc = tc.nc
+    x_view = inputs.rearrange("(j p) u k -> p j (u k)", p=P)
+    w_view = w_ih.flatten_outer_dims().rearrange("(c p) k -> p c k", p=P)
+    h_view = hidden.rearrange("(j p) u h -> p j (u h)", p=P)
+    whh_view = w_hh.flatten_outer_dims().rearrange("(c p) k -> p c k", p=P)
+    out_view = out.rearrange("(j p) u h -> p j (u h)", p=P)
+
+    with ExitStack() as ctx:
+        const = ctx.enter_context(tc.tile_pool(name="const", bufs=1))
+        stage = ctx.enter_context(tc.tile_pool(name="stage", bufs=2))
+        quant = ctx.enter_context(tc.tile_pool(name="quant", bufs=3))
+        work = ctx.enter_context(tc.tile_pool(name="work", bufs=3))
+        ps_t = ctx.enter_context(tc.psum_pool(name="ps_t", bufs=3))
+        ps_g = ctx.enter_context(tc.psum_pool(name="ps_g", bufs=4))
+        ps_o = ctx.enter_context(tc.psum_pool(name="ps_o", bufs=1))
+
+        warm = const.tile([P, 2], F32, name="warm")
+        nc.vector.memset(warm[:], 0.0)
+        nc.scalar.activation(out=warm[:, 1:2], in_=warm[:, 0:1], func=ACT.Sigmoid)
+        bias_rows = const.tile([P, P], BF16, name="bias_rows")
+        nc.vector.memset(bias_rows[:], 0.0)
+        nc.scalar.dma_start(out=bias_rows[0:48, :], in_=b_ih.rearrange("u (t h) -> (u t) h", h=P))
+        nc.scalar.dma_start(out=bias_rows[48:96, :], in_=b_hh.rearrange("u (t h) -> (u t) h", h=P))
+        ident_f = const.tile([P, P], F32, name="ident_f")
+        masks.make_identity(nc, ident_f[:])
+        ident_b = const.tile([P, P], BF16, name="ident_b")
+        masks.make_identity(nc, ident_b[:])
+
+        x_nat = [const.tile([P, 2, 2 * I], BF16, name="x_nat%d" % q) for q in range(NPAIR)]
+        w_nat = [const.tile([P, 6, I], BF16, name="w_nat%d" % q) for q in range(NPAIR)]
+        h_nat = [const.tile([P, 2, 8 * H], BF16, name="h_nat%d" % q) for q in range(2)]
+        whh_nat = [const.tile([P, 12, H], BF16, name="whh_nat%d" % q) for q in range(4)]
+
+        def load_x(q):
+            nc.sync.dma_start(out=x_nat[q][:], in_=x_view[:, :, q * 2 * I:(q + 1) * 2 * I])
+
+        def load_w(q):
+            nc.sync.dma_start(out=w_nat[q][:], in_=w_view[:, q * 6:(q + 1) * 6, :])
+
+        def load_h(q):
+            nc.sync.dma_start(out=h_nat[q][:], in_=h_view[:, :, q * 8 * H:(q + 1) * 8 * H])
+
+        def load_whh(q):
+            nc.sync.dma_start(out=whh_nat[q][:], in_=whh_view[:, q * 12:(q + 1) * 12, :])
+
+        load_x(0)
+        load_w(0)
+        load_h(0)
+        load_whh(0)
+        load_x(1)
+        load_w(1)
+        load_x(2)
+        load_w(2)
+        load_whh(1)
+        load_x(3)
+        load_w(3)
+        load_h(1)
+        load_whh(2)
+        load_x(4)
+        load_w(4)
+        load_x(5)
+        load_w(5)
+        load_whh(3)
+        load_x(6)
+        load_w(6)
+        load_x(7)
+        load_w(7)
+
+        bias_ps = ps_t.tile([P, 8, P], BF16, tag="T", name="bias_ps")
+        nc.tensor.transpose(bias_ps[:, 0, :], bias_rows[:], ident_b[:])
+        bias_cols = const.tile([P, P], F32, name="bias_cols")
+        nc.vector.tensor_copy(out=bias_cols[:], in_=bias_ps[:, 0, :])
+        bsum = const.tile([P, 48], F32, name="bsum")
+        nc.vector.tensor_tensor(out=bsum[:], in0=bias_cols[:, 0:48], in1=bias_cols[:, 48:96], op=ALU.add)
+        nbsum = const.tile([P, 48], F32, name="nbsum")
+        nc.vector.tensor_scalar_mul(out=nbsum[:], in0=bsum[:], scalar1=-1.0)
+
+        def word_bank(slices, dst_words, copy):
+            bank = ps_t.tile([P, 2, 2, P], F32, tag="T", name="bank")
+            for a in range(2):
+                for half in range(2):
+                    nc.tensor.transpose(bank[:, a, half, :], slices[a][:, half * P:(half + 1) * P], ident_f[:])
+            copy(out=dst_words.rearrange("p (a c w) -> p a c w", a=2, c=P, w=2),
+                 in_=bank[:].rearrange("p a w c -> p a c w"))
+
+        codes = {}
+
+        def quantise(key, grouped, width):
+            c = quant.tile([P, width // 4], U32, name="c_" + key, align_bytes=64)
+            s = quant.tile([P, width // 4], U8, name="s_" + key, align_bytes=64)
+            nc.vector.quantize_mx(out=c[:].bitcast(FP8X4), scales=s[:], in_=grouped[:])
+            return c, s
+
+        def prep(q):
+            gx = stage.tile([P, 2048], BF16, name="gx", align_bytes=64)
+            gw = stage.tile([P, 2048], BF16, name="gw", align_bytes=64)
+            gn = stage.tile([P, 1024], BF16, name="gn", align_bytes=64)
+            gxf = gx[:].bitcast(F32)
+            gwf = gw[:].bitcast(F32)
+            gnf = gn[:].bitcast(F32)
+            for l in range(2):
+                word_bank([x_nat[q][:, j, l * I:(l + 1) * I].bitcast(F32) for j in range(2)],
+                          gxf[:, l * 512:(l + 1) * 512], nc.scalar.copy)
+            for l in range(2):
+                word_bank([w_nat[q][:, l * 3 + t, :].bitcast(F32) for t in range(2)],
+                          gwf[:, l * 512:(l + 1) * 512], nc.scalar.copy)
+            word_bank([w_nat[q][:, l * 3 + 2, :].bitcast(F32) for l in range(2)], gnf, nc.vector.tensor_copy)
+            codes[("x", q)] = quantise("x", gx, 2048)
+            codes[("w", q)] = quantise("w", gw, 2048)
+            codes[("n", q)] = quantise("n", gn, 1024)
+
+        h_t = {}
+        whh_t = {}
+
+        def prep_h(quad):
+            src = h_nat[quad // 2]
+            bank = ps_t.tile([P, 8, P], BF16, tag="T", name="hbank")
+            for i in range(4):
+                col = ((quad % 2) * 4 + i) * H
+                for j in range(2):
+                    nc.tensor.transpose(bank[:, i * 2 + j, :], src[:, j, col:col + H], ident_b[:])
+            t = const.tile([P, 8, P], BF16, name="h_t%d" % quad)
+            nc.vector.tensor_copy(out=t[:], in_=bank[:])
+            h_t[quad] = t
+
+        def prep_whh(q):
+            src = whh_nat[q // 2]
+            bank = ps_t.tile([P, 8, P], BF16, tag="T", name="wbank")
+            for i in range(6):
+                nc.tensor.transpose(bank[:, i, :], src[:, (q % 2) * 6 + i, :], ident_b[:])
+            t = const.tile([P, 6, P], BF16, name="whh_t%d" % q)
+            nc.scalar.copy(out=t[:], in_=bank[:, 0:6, :])
+            whh_t[q] = t
+
+        def h_cols(u):
+            return h_t[u // 4][:, (u % 4) * 2:(u % 4) * 2 + 2, :].rearrange("p j b -> p (j b)")
+
+        def unit(u, o_ps):
+            q, l = u // 2, u % 2
+            cx, sx = codes[("x", q)]
+            cw, sw = codes[("w", q)]
+            cn, sn = codes[("n", q)]
+            ht = h_cols(u)
+            wt = whh_t[q]
+            xs = slice(l * 256, (l + 1) * 256)
+            h1 = ps_g.tile([P, 512], F32, tag="G", name="h1")
+            x1 = ps_g.tile([P, 512], F32, tag="G", name="x1")
+            nn = ps_g.tile([P, 512], F32, tag="G", name="nn")
+            for t in range(2):
+                nc.tensor.matmul(out=h1[:, t * 256:(t + 1) * 256], lhsT=wt[:, l * 3 + t, :], rhs=ht,
+                                 start=True, stop=True)
+            nc.tensor.matmul(out=nn[:, 0:256], lhsT=wt[:, l * 3 + 2, :], rhs=ht, start=True, stop=True)
+            for t in range(2):
+                ws = slice(l * 256 + t * P, l * 256 + (t + 1) * P)
+                nc.tensor.matmul_mx(out=x1[:, t * 256:(t + 1) * 256],
+                                    lhsT=cw[:, ws].bitcast(FP8X4), lhsT_scale=sw[:, ws],
+                                    rhs=cx[:, xs].bitcast(FP8X4), rhs_scale=sx[:, xs],
+                                    start=True, stop=True)
+            ws = slice(l * P, (l + 1) * P)
+            nc.tensor.matmul_mx(out=nn[:, 256:512],
+                                lhsT=cn[:, ws].bitcast(FP8X4), lhsT_scale=sn[:, ws],
+                                rhs=cx[:, xs].bitcast(FP8X4), rhs_scale=sx[:, xs],
+                                start=True, stop=True)
+
+            hrz = work.tile([P, 512], F32, name="hrz")
+            nc.scalar.copy(out=hrz[:], in_=h1[:])
+            prz = work.tile([P, 512], F32, name="prz")
+            nc.vector.tensor_tensor(out=prz[:], in0=x1[:], in1=hrz[:], op=ALU.add)
+            r = work.tile([P, 256], F32, name="r")
+            nc.scalar.activation(out=r[:], in_=prz[:, 0:256], func=ACT.Sigmoid,
+                                 bias=bsum[:, 3 * u:3 * u + 1], scale=1.0)
+            zc = work.tile([P, 256], F32, name="zc")
+            nc.scalar.activation(out=zc[:], in_=prz[:, 256:512], func=ACT.Sigmoid,
+                                 bias=nbsum[:, 3 * u + 1:3 * u + 2], scale=-1.0)
+            m = work.tile([P, 256], F32, name="m")
+            nc.vector.scalar_tensor_tensor(out=m[:], in0=nn[:, 0:256],
+                                           scalar=bias_cols[:, 48 + 3 * u + 2:48 + 3 * u + 3],
+                                           in1=r[:], op0=ALU.add, op1=ALU.mult)
+            v = work.tile([P, 256], F32, name="v")
+            nc.vector.tensor_tensor(out=v[:], in0=nn[:, 256:512], in1=m[:], op=ALU.add)
+            n = work.tile([P, 256], F32, name="n")
+            nc.scalar.activation(out=n[:], in_=v[:], func=ACT.Tanh,
+                                 bias=bias_cols[:, 3 * u + 2:3 * u + 3], scale=1.0)
+            d = work.tile([P, 256], F32, name="d")
+            nc.gpsimd.tensor_tensor(out=d[:], in0=n[:], in1=ht, op=ALU.subtract)
+            f = work.tile([P, 256], F32, name="f")
+            nc.gpsimd.tensor_tensor(out=f[:], in0=zc[:], in1=d[:], op=ALU.mult)
+            for j in range(2):
+                nc.tensor.transpose(o_ps[:, j, l, :], f[:, j * P:(j + 1) * P], ident_f[:])
+
+        def finish(q, o_ps):
+            o_sb = const.tile([P, 2, 2 * H], F32, name="o_sb%d" % q)
+            col = (q % 4) * 2 * H
+            nc.vector.tensor_tensor(out=o_sb[:], in0=o_ps[:].rearrange("p j l h -> p j (l h)"),
+                                    in1=h_nat[q // 4][:, :, col:col + 2 * H], op=ALU.add)
+            nc.sync.dma_start(out=out_view[:, :, q * 2 * H:(q + 1) * 2 * H], in_=o_sb[:])
+
+        prep(0)
+        prep_h(0)
+        prep_whh(0)
+        for q in range(NPAIR):
+            if q + 1 < NPAIR:
+                prep(q + 1)
+                if (q + 1) % 2 == 0:
+                    prep_h((q + 1) // 2)
+                prep_whh(q + 1)
+            o_ps = ps_o.tile([P, 2, 2, P], F32, tag="O", name="o_ps")
+            unit(2 * q, o_ps)
+            unit(2 * q + 1, o_ps)
+            finish(q, o_ps)

@@ -1,9 +1,7 @@
 from contextlib import ExitStack
 
-import concourse.bass as bass
 import concourse.masks as masks
 import concourse.mybir as mybir
-import concourse.tile as tile
 
 F32 = mybir.dt.float32
 BF16 = mybir.dt.bfloat16
@@ -15,8 +13,37 @@ ALU = mybir.AluOpType
 
 P = 128
 B, U, I, H = 256, 16, 512, 128
-NPAIR = U // 2
 FLOPS = 2 * B * U * 3 * H * (I + H)
+
+ORDER = (
+    ("ex", 1),
+    ("Epl", -1),
+    ("ewrz", 1),
+    ("S1", 0),
+    ("Emx", -1),
+    ("Tx", 2),
+    ("Twrz", 2),
+    ("ewn", 1),
+    ("S2", -1),
+    ("S4", -2),
+    ("ehh", 1),
+    ("Q1", 1),
+    ("Q2", 1),
+    ("S3", -2),
+    ("Tf", -3),
+    ("Apl", 1),
+    ("V2", -1),
+    ("Twn", 2),
+    ("Thh", 2),
+    ("G1", -2),
+    ("V1", 0),
+    ("V3", -1),
+    ("G2", -2),
+    ("Amx", 1),
+    ("V4", -3),
+    ("st", -3),
+)
+LOADS = ("x0", "w0", "h0", "g0", "x1", "w1", "X1", "W1", "g1", "X2", "W2", "h1", "g2", "X3", "W3", "g3", "X4", "W4", "h2", "g4", "X5", "W5", "g5", "X6", "W6", "h3", "g6", "X7", "W7", "g7")
 
 
 def tile_grouptorchgru_kernel(tc, inputs, hidden, w_ih, w_hh, b_ih, b_hh, out):
@@ -32,63 +59,54 @@ def tile_grouptorchgru_kernel(tc, inputs, hidden, w_ih, w_hh, b_ih, b_hh, out):
         stage = ctx.enter_context(tc.tile_pool(name="stage", bufs=2))
         quant = ctx.enter_context(tc.tile_pool(name="quant", bufs=3))
         work = ctx.enter_context(tc.tile_pool(name="work", bufs=3))
-        ps_t = ctx.enter_context(tc.psum_pool(name="ps_t", bufs=3))
-        ps_g = ctx.enter_context(tc.psum_pool(name="ps_g", bufs=4))
-        ps_o = ctx.enter_context(tc.psum_pool(name="ps_o", bufs=1))
+        ps = ctx.enter_context(tc.psum_pool(name="ps", bufs=1))
+        ctx.enter_context(tc.manual_schedule())
 
+        bias_rows = const.tile([P, P], BF16, name="bias_rows")
+        nc.scalar.dma_start(out=bias_rows[0:48, :], in_=b_ih.rearrange("u (t h) -> (u t) h", h=P))
+        nc.scalar.dma_start(out=bias_rows[48:96, :], in_=b_hh.rearrange("u (t h) -> (u t) h", h=P))
+        nc.vector.memset(bias_rows[96:128, :], 0.0)
         warm = const.tile([P, 2], F32, name="warm")
         nc.vector.memset(warm[:], 0.0)
         nc.scalar.activation(out=warm[:, 1:2], in_=warm[:, 0:1], func=ACT.Sigmoid)
-        bias_rows = const.tile([P, P], BF16, name="bias_rows")
-        nc.vector.memset(bias_rows[:], 0.0)
-        nc.scalar.dma_start(out=bias_rows[0:48, :], in_=b_ih.rearrange("u (t h) -> (u t) h", h=P))
-        nc.scalar.dma_start(out=bias_rows[48:96, :], in_=b_hh.rearrange("u (t h) -> (u t) h", h=P))
-        ident_f = const.tile([P, P], F32, name="ident_f")
-        masks.make_identity(nc, ident_f[:])
         ident_b = const.tile([P, P], BF16, name="ident_b")
         masks.make_identity(nc, ident_b[:])
+        ident_f = const.tile([P, P], F32, name="ident_f")
+        masks.make_identity(nc, ident_f[:])
 
-        x_nat = [const.tile([P, 2, 2 * I], BF16, name="x_nat%d" % q) for q in range(NPAIR)]
-        w_nat = [const.tile([P, 6, I], BF16, name="w_nat%d" % q) for q in range(NPAIR)]
-        h_nat = [const.tile([P, 2, 8 * H], BF16, name="h_nat%d" % q) for q in range(2)]
-        whh_nat = [const.tile([P, 12, H], BF16, name="whh_nat%d" % q) for q in range(4)]
+        src = {}
+        for item in LOADS:
+            kind, k = item[0], int(item[1:])
+            if kind == "x":
+                t = const.tile([P, 2, I], BF16, name="x_u%d" % k)
+                nc.sync.dma_start(out=t[:], in_=x_view[:, :, k * I:(k + 1) * I])
+                src[("x", k)] = t[:]
+            elif kind == "X":
+                t = const.tile([P, 2, 2 * I], BF16, name="x_p%d" % k)
+                nc.sync.dma_start(out=t[:], in_=x_view[:, :, 2 * k * I:(2 * k + 2) * I])
+                for l in range(2):
+                    src[("x", 2 * k + l)] = t[:, :, l * I:(l + 1) * I]
+            elif kind == "w":
+                t = const.tile([P, 3, I], BF16, name="w_u%d" % k)
+                nc.sync.dma_start(out=t[:], in_=w_view[:, 3 * k:3 * k + 3, :])
+                src[("w", k)] = t[:]
+            elif kind == "W":
+                t = const.tile([P, 6, I], BF16, name="w_p%d" % k)
+                nc.sync.dma_start(out=t[:], in_=w_view[:, 6 * k:6 * k + 6, :])
+                for l in range(2):
+                    src[("w", 2 * k + l)] = t[:, 3 * l:3 * l + 3, :]
+            elif kind == "h":
+                t = const.tile([P, 2, 4 * H], BF16, name="h_q%d" % k)
+                nc.sync.dma_start(out=t[:], in_=h_view[:, :, 4 * k * H:(4 * k + 4) * H])
+                for l in range(4):
+                    src[("h", 4 * k + l)] = t[:, :, l * H:(l + 1) * H]
+            elif kind == "g":
+                t = const.tile([P, 6, H], BF16, name="g_p%d" % k)
+                nc.sync.dma_start(out=t[:], in_=whh_view[:, 6 * k:6 * k + 6, :])
+                for l in range(2):
+                    src[("g", 2 * k + l)] = t[:, 3 * l:3 * l + 3, :]
 
-        def load_x(q):
-            nc.sync.dma_start(out=x_nat[q][:], in_=x_view[:, :, q * 2 * I:(q + 1) * 2 * I])
-
-        def load_w(q):
-            nc.sync.dma_start(out=w_nat[q][:], in_=w_view[:, q * 6:(q + 1) * 6, :])
-
-        def load_h(q):
-            nc.sync.dma_start(out=h_nat[q][:], in_=h_view[:, :, q * 8 * H:(q + 1) * 8 * H])
-
-        def load_whh(q):
-            nc.sync.dma_start(out=whh_nat[q][:], in_=whh_view[:, q * 12:(q + 1) * 12, :])
-
-        load_x(0)
-        load_w(0)
-        load_h(0)
-        load_whh(0)
-        load_x(1)
-        load_w(1)
-        load_x(2)
-        load_w(2)
-        load_whh(1)
-        load_x(3)
-        load_w(3)
-        load_h(1)
-        load_whh(2)
-        load_x(4)
-        load_w(4)
-        load_x(5)
-        load_w(5)
-        load_whh(3)
-        load_x(6)
-        load_w(6)
-        load_x(7)
-        load_w(7)
-
-        bias_ps = ps_t.tile([P, 8, P], BF16, tag="T", name="bias_ps")
+        bias_ps = ps.tile([P, 5, P], BF16, tag="thh", name="bias_ps")
         nc.tensor.transpose(bias_ps[:, 0, :], bias_rows[:], ident_b[:])
         bias_cols = const.tile([P, P], F32, name="bias_cols")
         nc.vector.tensor_copy(out=bias_cols[:], in_=bias_ps[:, 0, :])
@@ -97,136 +115,196 @@ def tile_grouptorchgru_kernel(tc, inputs, hidden, w_ih, w_hh, b_ih, b_hh, out):
         nbsum = const.tile([P, 48], F32, name="nbsum")
         nc.vector.tensor_scalar_mul(out=nbsum[:], in0=bsum[:], scalar1=-1.0)
 
-        def word_bank(slices, dst_words, copy):
-            bank = ps_t.tile([P, 2, 2, P], F32, tag="T", name="bank")
-            for a in range(2):
+        tl = {}
+
+        def words(ap):
+            return ap.bitcast(F32)
+
+        def grouped1(u):
+            if ("g1", u) not in tl:
+                tl[("g1", u)] = stage.tile([P, 2048], BF16, name="g1", align_bytes=64)
+            return tl[("g1", u)]
+
+        def s_tx(u):
+            bank = ps.tile([P, 2, 2, P], F32, tag="tx", name="tx")
+            for j in range(2):
                 for half in range(2):
-                    nc.tensor.transpose(bank[:, a, half, :], slices[a][:, half * P:(half + 1) * P], ident_f[:])
-            copy(out=dst_words.rearrange("p (a c w) -> p a c w", a=2, c=P, w=2),
-                 in_=bank[:].rearrange("p a w c -> p a c w"))
+                    nc.tensor.transpose(bank[:, j, half, :],
+                                        words(src[("x", u)][:, j, :])[:, half * P:(half + 1) * P], ident_f[:])
+            tl[("tx", u)] = bank
 
-        codes = {}
+        def s_ex(u):
+            nc.scalar.copy(out=words(grouped1(u)[:, 0:1024]).rearrange("p (a c w) -> p a c w", a=2, c=P, w=2),
+                           in_=tl[("tx", u)][:].rearrange("p a w c -> p a c w"))
 
-        def quantise(key, grouped, width):
-            c = quant.tile([P, width // 4], U32, name="c_" + key, align_bytes=64)
-            s = quant.tile([P, width // 4], U8, name="s_" + key, align_bytes=64)
-            nc.vector.quantize_mx(out=c[:].bitcast(FP8X4), scales=s[:], in_=grouped[:])
-            return c, s
-
-        def prep(q):
-            gx = stage.tile([P, 2048], BF16, name="gx", align_bytes=64)
-            gw = stage.tile([P, 2048], BF16, name="gw", align_bytes=64)
-            gn = stage.tile([P, 1024], BF16, name="gn", align_bytes=64)
-            gxf = gx[:].bitcast(F32)
-            gwf = gw[:].bitcast(F32)
-            gnf = gn[:].bitcast(F32)
-            for l in range(2):
-                word_bank([x_nat[q][:, j, l * I:(l + 1) * I].bitcast(F32) for j in range(2)],
-                          gxf[:, l * 512:(l + 1) * 512], nc.scalar.copy)
-            for l in range(2):
-                word_bank([w_nat[q][:, l * 3 + t, :].bitcast(F32) for t in range(2)],
-                          gwf[:, l * 512:(l + 1) * 512], nc.scalar.copy)
-            word_bank([w_nat[q][:, l * 3 + 2, :].bitcast(F32) for l in range(2)], gnf, nc.vector.tensor_copy)
-            codes[("x", q)] = quantise("x", gx, 2048)
-            codes[("w", q)] = quantise("w", gw, 2048)
-            codes[("n", q)] = quantise("n", gn, 1024)
-
-        h_t = {}
-        whh_t = {}
-
-        def prep_h(quad):
-            src = h_nat[quad // 2]
-            bank = ps_t.tile([P, 8, P], BF16, tag="T", name="hbank")
-            for i in range(4):
-                col = ((quad % 2) * 4 + i) * H
-                for j in range(2):
-                    nc.tensor.transpose(bank[:, i * 2 + j, :], src[:, j, col:col + H], ident_b[:])
-            t = const.tile([P, 8, P], BF16, name="h_t%d" % quad)
-            nc.vector.tensor_copy(out=t[:], in_=bank[:])
-            h_t[quad] = t
-
-        def prep_whh(q):
-            src = whh_nat[q // 2]
-            bank = ps_t.tile([P, 8, P], BF16, tag="T", name="wbank")
-            for i in range(6):
-                nc.tensor.transpose(bank[:, i, :], src[:, (q % 2) * 6 + i, :], ident_b[:])
-            t = const.tile([P, 6, P], BF16, name="whh_t%d" % q)
-            nc.scalar.copy(out=t[:], in_=bank[:, 0:6, :])
-            whh_t[q] = t
-
-        def h_cols(u):
-            return h_t[u // 4][:, (u % 4) * 2:(u % 4) * 2 + 2, :].rearrange("p j b -> p (j b)")
-
-        def unit(u, o_ps):
-            q, l = u // 2, u % 2
-            cx, sx = codes[("x", q)]
-            cw, sw = codes[("w", q)]
-            cn, sn = codes[("n", q)]
-            ht = h_cols(u)
-            wt = whh_t[q]
-            xs = slice(l * 256, (l + 1) * 256)
-            h1 = ps_g.tile([P, 512], F32, tag="G", name="h1")
-            x1 = ps_g.tile([P, 512], F32, tag="G", name="x1")
-            nn = ps_g.tile([P, 512], F32, tag="G", name="nn")
+        def s_twrz(u):
+            bank = ps.tile([P, 2, 2, P], F32, tag="twrz", name="twrz")
             for t in range(2):
-                nc.tensor.matmul(out=h1[:, t * 256:(t + 1) * 256], lhsT=wt[:, l * 3 + t, :], rhs=ht,
+                for half in range(2):
+                    nc.tensor.transpose(bank[:, t, half, :],
+                                        words(src[("w", u)][:, t, :])[:, half * P:(half + 1) * P], ident_f[:])
+            tl[("twrz", u)] = bank
+
+        def s_ewrz(u):
+            nc.scalar.copy(out=words(grouped1(u)[:, 1024:2048]).rearrange("p (a c w) -> p a c w", a=2, c=P, w=2),
+                           in_=tl[("twrz", u)][:].rearrange("p a w c -> p a c w"))
+
+        def s_twn(u):
+            bank = ps.tile([P, 2, P], F32, tag="twn", name="twn")
+            for half in range(2):
+                nc.tensor.transpose(bank[:, half, :],
+                                    words(src[("w", u)][:, 2, :])[:, half * P:(half + 1) * P], ident_f[:])
+            tl[("twn", u)] = bank
+
+        def s_ewn(u):
+            g2 = stage.tile([P, 512], BF16, name="g2", align_bytes=64)
+            nc.vector.tensor_copy(out=words(g2[:]).rearrange("p (c w) -> p c w", c=P, w=2),
+                                  in_=tl[("twn", u)][:].rearrange("p w c -> p c w"))
+            tl[("g2", u)] = g2
+
+        def s_thh(u):
+            bank = ps.tile([P, 5, P], BF16, tag="thh", name="thh")
+            for j in range(2):
+                nc.tensor.transpose(bank[:, j, :], src[("h", u)][:, j, :], ident_b[:])
+            for t in range(3):
+                nc.tensor.transpose(bank[:, 2 + t, :], src[("g", u)][:, t, :], ident_b[:])
+            tl[("thh", u)] = bank
+
+        def s_ehh(u):
+            hh = const.tile([P, 5, P], BF16, name="hh%d" % u)
+            if u % 2 == 0:
+                nc.scalar.copy(out=hh[:], in_=tl[("thh", u)][:])
+            else:
+                nc.vector.tensor_copy(out=hh[:], in_=tl[("thh", u)][:])
+            tl[("hh", u)] = hh
+
+        def h_t(u):
+            return tl[("hh", u)][:, 0:2, :].rearrange("p j b -> p (j b)")
+
+        def s_q1(u):
+            c = quant.tile([P, 512], U32, name="c1", align_bytes=64)
+            s = quant.tile([P, 512], U8, name="s1", align_bytes=64)
+            nc.vector.quantize_mx(out=c[:].bitcast(FP8X4), scales=s[:], in_=tl[("g1", u)][:])
+            tl[("q1", u)] = (c, s)
+
+        def s_q2(u):
+            c = quant.tile([P, P], U32, name="c2", align_bytes=64)
+            s = quant.tile([P, P], U8, name="s2", align_bytes=64)
+            nc.vector.quantize_mx(out=c[:].bitcast(FP8X4), scales=s[:], in_=tl[("g2", u)][:])
+            tl[("q2", u)] = (c, s)
+
+        def s_apl(u):
+            h1 = ps.tile([P, 512], F32, tag="h1", name="h1")
+            for t in range(2):
+                nc.tensor.matmul(out=h1[:, t * 256:(t + 1) * 256], lhsT=tl[("hh", u)][:, 2 + t, :], rhs=h_t(u),
                                  start=True, stop=True)
-            nc.tensor.matmul(out=nn[:, 0:256], lhsT=wt[:, l * 3 + 2, :], rhs=ht, start=True, stop=True)
+            tl[("h1", u)] = h1
+
+        def s_amx(u):
+            x1 = ps.tile([P, 512], F32, tag="x1", name="x1")
+            c, s = tl[("q1", u)]
             for t in range(2):
-                ws = slice(l * 256 + t * P, l * 256 + (t + 1) * P)
+                ws = slice(256 + t * P, 256 + (t + 1) * P)
                 nc.tensor.matmul_mx(out=x1[:, t * 256:(t + 1) * 256],
-                                    lhsT=cw[:, ws].bitcast(FP8X4), lhsT_scale=sw[:, ws],
-                                    rhs=cx[:, xs].bitcast(FP8X4), rhs_scale=sx[:, xs],
+                                    lhsT=c[:, ws].bitcast(FP8X4), lhsT_scale=s[:, ws],
+                                    rhs=c[:, 0:256].bitcast(FP8X4), rhs_scale=s[:, 0:256],
                                     start=True, stop=True)
-            ws = slice(l * P, (l + 1) * P)
-            nc.tensor.matmul_mx(out=nn[:, 256:512],
-                                lhsT=cn[:, ws].bitcast(FP8X4), lhsT_scale=sn[:, ws],
-                                rhs=cx[:, xs].bitcast(FP8X4), rhs_scale=sx[:, xs],
+            tl[("x1", u)] = x1
+
+        def s_epl(u):
+            nn = ps.tile([P, 512], F32, tag="nn", name="nn")
+            nc.tensor.matmul(out=nn[:, 0:256], lhsT=tl[("hh", u)][:, 4, :], rhs=h_t(u), start=True, stop=True)
+            tl[("nn", u)] = nn
+
+        def s_emx(u):
+            c, s = tl[("q1", u)]
+            cn, sn = tl[("q2", u)]
+            nc.tensor.matmul_mx(out=tl[("nn", u)][:, 256:512],
+                                lhsT=cn[:].bitcast(FP8X4), lhsT_scale=sn[:],
+                                rhs=c[:, 0:256].bitcast(FP8X4), rhs_scale=s[:, 0:256],
                                 start=True, stop=True)
 
+        def s_s1(u):
             hrz = work.tile([P, 512], F32, name="hrz")
-            nc.scalar.copy(out=hrz[:], in_=h1[:])
+            nc.scalar.copy(out=hrz[:], in_=tl[("h1", u)][:])
+            tl[("hrz", u)] = hrz
+
+        def s_v1(u):
             prz = work.tile([P, 512], F32, name="prz")
-            nc.vector.tensor_tensor(out=prz[:], in0=x1[:], in1=hrz[:], op=ALU.add)
+            nc.vector.tensor_tensor(out=prz[:], in0=tl[("x1", u)][:], in1=tl[("hrz", u)][:], op=ALU.add)
+            tl[("prz", u)] = prz
+
+        def s_s2(u):
             r = work.tile([P, 256], F32, name="r")
-            nc.scalar.activation(out=r[:], in_=prz[:, 0:256], func=ACT.Sigmoid,
+            nc.scalar.activation(out=r[:], in_=tl[("prz", u)][:, 0:256], func=ACT.Sigmoid,
                                  bias=bsum[:, 3 * u:3 * u + 1], scale=1.0)
+            tl[("r", u)] = r
+
+        def s_s3(u):
             zc = work.tile([P, 256], F32, name="zc")
-            nc.scalar.activation(out=zc[:], in_=prz[:, 256:512], func=ACT.Sigmoid,
+            nc.scalar.activation(out=zc[:], in_=tl[("prz", u)][:, 256:512], func=ACT.Sigmoid,
                                  bias=nbsum[:, 3 * u + 1:3 * u + 2], scale=-1.0)
+            tl[("zc", u)] = zc
+
+        def s_v2(u):
             m = work.tile([P, 256], F32, name="m")
-            nc.vector.scalar_tensor_tensor(out=m[:], in0=nn[:, 0:256],
+            nc.vector.scalar_tensor_tensor(out=m[:], in0=tl[("nn", u)][:, 0:256],
                                            scalar=bias_cols[:, 48 + 3 * u + 2:48 + 3 * u + 3],
-                                           in1=r[:], op0=ALU.add, op1=ALU.mult)
+                                           in1=tl[("r", u)][:], op0=ALU.add, op1=ALU.mult)
+            tl[("m", u)] = m
+
+        def s_v3(u):
             v = work.tile([P, 256], F32, name="v")
-            nc.vector.tensor_tensor(out=v[:], in0=nn[:, 256:512], in1=m[:], op=ALU.add)
+            nc.vector.tensor_tensor(out=v[:], in0=tl[("nn", u)][:, 256:512], in1=tl[("m", u)][:], op=ALU.add)
+            tl[("v", u)] = v
+
+        def s_s4(u):
             n = work.tile([P, 256], F32, name="n")
-            nc.scalar.activation(out=n[:], in_=v[:], func=ACT.Tanh,
+            nc.scalar.activation(out=n[:], in_=tl[("v", u)][:], func=ACT.Tanh,
                                  bias=bias_cols[:, 3 * u + 2:3 * u + 3], scale=1.0)
+            tl[("n", u)] = n
+
+        def blend_engine(u):
+            if False:
+                return nc.vector
+            return nc.gpsimd
+
+        def s_g1(u):
             d = work.tile([P, 256], F32, name="d")
-            nc.gpsimd.tensor_tensor(out=d[:], in0=n[:], in1=ht, op=ALU.subtract)
+            blend_engine(u).tensor_tensor(out=d[:], in0=tl[("n", u)][:], in1=h_t(u), op=ALU.subtract)
+            tl[("d", u)] = d
+
+        def s_g2(u):
             f = work.tile([P, 256], F32, name="f")
-            nc.gpsimd.tensor_tensor(out=f[:], in0=zc[:], in1=d[:], op=ALU.mult)
+            blend_engine(u).tensor_tensor(out=f[:], in0=tl[("zc", u)][:], in1=tl[("d", u)][:], op=ALU.mult)
+            tl[("f", u)] = f
+
+        def s_tf(u):
+            o_ps = ps.tile([P, 2, P], F32, tag="o", name="o_ps")
             for j in range(2):
-                nc.tensor.transpose(o_ps[:, j, l, :], f[:, j * P:(j + 1) * P], ident_f[:])
+                nc.tensor.transpose(o_ps[:, j, :], tl[("f", u)][:, j * P:(j + 1) * P], ident_f[:])
+            tl[("o", u)] = o_ps
 
-        def finish(q, o_ps):
-            o_sb = const.tile([P, 2, 2 * H], F32, name="o_sb%d" % q)
-            col = (q % 4) * 2 * H
-            nc.vector.tensor_tensor(out=o_sb[:], in0=o_ps[:].rearrange("p j l h -> p j (l h)"),
-                                    in1=h_nat[q // 4][:, :, col:col + 2 * H], op=ALU.add)
-            nc.sync.dma_start(out=out_view[:, :, q * 2 * H:(q + 1) * 2 * H], in_=o_sb[:])
+        def s_v4(u):
+            q, l = u // 2, u % 2
+            if ("o_sb", q) not in tl:
+                tl[("o_sb", q)] = const.tile([P, 2, 2 * H], F32, name="o_sb%d" % q)
+            nc.vector.tensor_tensor(out=tl[("o_sb", q)][:, :, l * H:(l + 1) * H], in0=tl[("o", u)][:],
+                                    in1=src[("h", u)], op=ALU.add)
 
-        prep(0)
-        prep_h(0)
-        prep_whh(0)
-        for q in range(NPAIR):
-            if q + 1 < NPAIR:
-                prep(q + 1)
-                if (q + 1) % 2 == 0:
-                    prep_h((q + 1) // 2)
-                prep_whh(q + 1)
-            o_ps = ps_o.tile([P, 2, 2, P], F32, tag="O", name="o_ps")
-            unit(2 * q, o_ps)
-            unit(2 * q + 1, o_ps)
-            finish(q, o_ps)
+        def s_st(u):
+            if u % 2 == 1:
+                q = u // 2
+                nc.sync.dma_start(out=out_view[:, :, q * 2 * H:(q + 1) * 2 * H], in_=tl[("o_sb", q)][:])
+
+        stages = {"Tx": s_tx, "ex": s_ex, "Twrz": s_twrz, "ewrz": s_ewrz, "Twn": s_twn, "ewn": s_ewn,
+                  "Thh": s_thh, "ehh": s_ehh, "Q1": s_q1, "Q2": s_q2, "Apl": s_apl, "Amx": s_amx,
+                  "Epl": s_epl, "Emx": s_emx, "S1": s_s1, "V1": s_v1, "S2": s_s2, "S3": s_s3,
+                  "V2": s_v2, "V3": s_v3, "S4": s_s4, "G1": s_g1, "G2": s_g2, "Tf": s_tf, "V4": s_v4,
+                  "st": s_st}
+
+        for i in range(-3, 22):
+            for name, off in ORDER:
+                u = i + off
+                if 0 <= u < U:
+                    stages[name](u)

@@ -13,298 +13,283 @@ ALU = mybir.AluOpType
 
 P = 128
 B, U, I, H = 256, 16, 512, 128
-FLOPS = 2 * B * U * 3 * H * (I + H)
-
-ORDER = (
-    ("ex", 1),
-    ("Epl", -1),
-    ("ewrz", 1),
-    ("S1", 0),
-    ("Emx", -1),
-    ("Tx", 2),
-    ("Twrz", 2),
-    ("ewn", 1),
-    ("S2", -1),
-    ("S4", -2),
-    ("ehh", 1),
-    ("Q1", 1),
-    ("Q2", 1),
-    ("S3", -2),
-    ("Tf", -3),
-    ("Apl", 1),
-    ("V2", -1),
-    ("Twn", 2),
-    ("Thh", 2),
-    ("G1", -2),
-    ("V1", 0),
-    ("V3", -1),
-    ("G2", -2),
-    ("Amx", 1),
-    ("V4", -3),
-    ("st", -3),
-)
-LOADS = ("x0", "w0", "h0", "g0", "x1", "w1", "X1", "W1", "g1", "X2", "W2", "h1", "g2", "X3", "W3", "g3", "X4", "W4", "h2", "g4", "X5", "W5", "g5", "X6", "W6", "h3", "g6", "X7", "W7", "g7")
+J = B // P
+GATES = 3
+PACK = 4
+WORDS = PACK // 2
+QUAD = 4
+FLOPS = 2 * B * U * GATES * H * (I + H)
 
 
 def tile_grouptorchgru_kernel(tc, inputs, hidden, w_ih, w_hh, b_ih, b_hh, out):
     nc = tc.nc
     x_view = inputs.rearrange("(j p) u k -> p j (u k)", p=P)
-    w_view = w_ih.flatten_outer_dims().rearrange("(c p) k -> p c k", p=P)
     h_view = hidden.rearrange("(j p) u h -> p j (u h)", p=P)
-    whh_view = w_hh.flatten_outer_dims().rearrange("(c p) k -> p c k", p=P)
     out_view = out.rearrange("(j p) u h -> p j (u h)", p=P)
+    w_view = w_ih.flatten_outer_dims().rearrange("(g p) k -> p g k", p=P)
+    whh_view = w_hh.flatten_outer_dims().rearrange("(g p) k -> p g k", p=P)
 
     with ExitStack() as ctx:
-        const = ctx.enter_context(tc.tile_pool(name="const", bufs=1))
+        keep = ctx.enter_context(tc.tile_pool(name="keep", bufs=1))
         stage = ctx.enter_context(tc.tile_pool(name="stage", bufs=2))
         quant = ctx.enter_context(tc.tile_pool(name="quant", bufs=3))
         work = ctx.enter_context(tc.tile_pool(name="work", bufs=3))
-        ps = ctx.enter_context(tc.psum_pool(name="ps", bufs=1))
+        psum = ctx.enter_context(tc.psum_pool(name="psum", bufs=1))
         ctx.enter_context(tc.manual_schedule())
 
-        bias_rows = const.tile([P, P], BF16, name="bias_rows")
-        nc.scalar.dma_start(out=bias_rows[0:48, :], in_=b_ih.rearrange("u (t h) -> (u t) h", h=P))
-        nc.scalar.dma_start(out=bias_rows[48:96, :], in_=b_hh.rearrange("u (t h) -> (u t) h", h=P))
-        nc.vector.memset(bias_rows[96:128, :], 0.0)
-        warm = const.tile([P, 2], F32, name="warm")
+        bias_rows = keep.tile([P, P], BF16, name="bias_rows")
+        nc.scalar.dma_start(out=bias_rows[0:U * GATES, :], in_=b_ih.rearrange("u (g h) -> (u g) h", h=H))
+        nc.scalar.dma_start(out=bias_rows[U * GATES:2 * U * GATES, :],
+                            in_=b_hh.rearrange("u (g h) -> (u g) h", h=H))
+        nc.vector.memset(bias_rows[2 * U * GATES:P, :], 0.0)
+        warm = keep.tile([P, 2], F32, name="warm")
         nc.vector.memset(warm[:], 0.0)
         nc.scalar.activation(out=warm[:, 1:2], in_=warm[:, 0:1], func=ACT.Sigmoid)
-        ident_b = const.tile([P, P], BF16, name="ident_b")
+        ident_b = keep.tile([P, P], BF16, name="ident_b")
         masks.make_identity(nc, ident_b[:])
-        ident_f = const.tile([P, P], F32, name="ident_f")
+        ident_f = keep.tile([P, P], F32, name="ident_f")
         masks.make_identity(nc, ident_f[:])
 
-        src = {}
-        for item in LOADS:
-            kind, k = item[0], int(item[1:])
-            if kind == "x":
-                t = const.tile([P, 2, I], BF16, name="x_u%d" % k)
-                nc.sync.dma_start(out=t[:], in_=x_view[:, :, k * I:(k + 1) * I])
-                src[("x", k)] = t[:]
-            elif kind == "X":
-                t = const.tile([P, 2, 2 * I], BF16, name="x_p%d" % k)
-                nc.sync.dma_start(out=t[:], in_=x_view[:, :, 2 * k * I:(2 * k + 2) * I])
-                for l in range(2):
-                    src[("x", 2 * k + l)] = t[:, :, l * I:(l + 1) * I]
-            elif kind == "w":
-                t = const.tile([P, 3, I], BF16, name="w_u%d" % k)
-                nc.sync.dma_start(out=t[:], in_=w_view[:, 3 * k:3 * k + 3, :])
-                src[("w", k)] = t[:]
-            elif kind == "W":
-                t = const.tile([P, 6, I], BF16, name="w_p%d" % k)
-                nc.sync.dma_start(out=t[:], in_=w_view[:, 6 * k:6 * k + 6, :])
-                for l in range(2):
-                    src[("w", 2 * k + l)] = t[:, 3 * l:3 * l + 3, :]
-            elif kind == "h":
-                t = const.tile([P, 2, 4 * H], BF16, name="h_q%d" % k)
-                nc.sync.dma_start(out=t[:], in_=h_view[:, :, 4 * k * H:(4 * k + 4) * H])
-                for l in range(4):
-                    src[("h", 4 * k + l)] = t[:, :, l * H:(l + 1) * H]
-            elif kind == "g":
-                t = const.tile([P, 6, H], BF16, name="g_p%d" % k)
-                nc.sync.dma_start(out=t[:], in_=whh_view[:, 6 * k:6 * k + 6, :])
-                for l in range(2):
-                    src[("g", 2 * k + l)] = t[:, 3 * l:3 * l + 3, :]
+        x_nat, w_nat, whh_nat, h_nat = [], [], [], []
+        for u in range(U):
+            x_nat.append(keep.tile([P, J, I], BF16, name="x_nat%d" % u))
+            nc.sync.dma_start(out=x_nat[u][:], in_=x_view[:, :, u * I:(u + 1) * I])
+            w_nat.append(keep.tile([P, GATES, I], BF16, name="w_nat%d" % u))
+            nc.sync.dma_start(out=w_nat[u][:], in_=w_view[:, u * GATES:(u + 1) * GATES, :])
+            if u % QUAD == 0:
+                h_nat.append(keep.tile([P, J, QUAD * H], BF16, name="h_nat%d" % (u // QUAD)))
+                nc.sync.dma_start(out=h_nat[u // QUAD][:], in_=h_view[:, :, u * H:(u + QUAD) * H])
+            whh_nat.append(keep.tile([P, GATES, H], BF16, name="whh_nat%d" % u))
+            nc.sync.dma_start(out=whh_nat[u][:], in_=whh_view[:, u * GATES:(u + 1) * GATES, :])
 
-        bias_ps = ps.tile([P, 5, P], BF16, tag="thh", name="bias_ps")
+        def hidden_rows(u):
+            return h_nat[u // QUAD][:, :, (u % QUAD) * H:(u % QUAD + 1) * H]
+
+        bias_ps = psum.tile([P, J + GATES, P], BF16, tag="hidden_t", name="bias_ps")
         nc.tensor.transpose(bias_ps[:, 0, :], bias_rows[:], ident_b[:])
-        bias_cols = const.tile([P, P], F32, name="bias_cols")
+        bias_cols = keep.tile([P, P], F32, name="bias_cols")
         nc.vector.tensor_copy(out=bias_cols[:], in_=bias_ps[:, 0, :])
-        bsum = const.tile([P, 48], F32, name="bsum")
-        nc.vector.tensor_tensor(out=bsum[:], in0=bias_cols[:, 0:48], in1=bias_cols[:, 48:96], op=ALU.add)
-        nbsum = const.tile([P, 48], F32, name="nbsum")
-        nc.vector.tensor_scalar_mul(out=nbsum[:], in0=bsum[:], scalar1=-1.0)
+        bias_sum = keep.tile([P, U * GATES], F32, name="bias_sum")
+        nc.vector.tensor_tensor(out=bias_sum[:], in0=bias_cols[:, 0:U * GATES],
+                                in1=bias_cols[:, U * GATES:2 * U * GATES], op=ALU.add)
+        bias_neg = keep.tile([P, U * GATES], F32, name="bias_neg")
+        nc.vector.tensor_scalar_mul(out=bias_neg[:], in0=bias_sum[:], scalar1=-1.0)
 
-        tl = {}
+        def column(table, index):
+            return table[:, index:index + 1]
 
-        def words(ap):
-            return ap.bitcast(F32)
+        made = {}
 
-        def grouped1(u):
-            if ("g1", u) not in tl:
-                tl[("g1", u)] = stage.tile([P, 2048], BF16, name="g1", align_bytes=64)
-            return tl[("g1", u)]
+        def absent(u):
+            return u < 0 or u >= U
 
-        def s_tx(u):
-            bank = ps.tile([P, 2, 2, P], F32, tag="tx", name="tx")
-            for j in range(2):
-                for half in range(2):
-                    nc.tensor.transpose(bank[:, j, half, :],
-                                        words(src[("x", u)][:, j, :])[:, half * P:(half + 1) * P], ident_f[:])
-            tl[("tx", u)] = bank
+        def transpose_words(bank, rows):
+            for a in range(len(rows)):
+                for w in range(WORDS):
+                    nc.tensor.transpose(bank[:, a, w, :], rows[a].bitcast(F32)[:, w * P:(w + 1) * P], ident_f[:])
 
-        def s_ex(u):
-            nc.scalar.copy(out=words(grouped1(u)[:, 0:1024]).rearrange("p (a c w) -> p a c w", a=2, c=P, w=2),
-                           in_=tl[("tx", u)][:].rearrange("p a w c -> p a c w"))
+        def interleave(copy, grouped, bank):
+            copy(out=grouped.bitcast(F32).rearrange("p (a c w) -> p a c w", c=P, w=WORDS),
+                 in_=bank[:].rearrange("p a w c -> p a c w"))
 
-        def s_twrz(u):
-            bank = ps.tile([P, 2, 2, P], F32, tag="twrz", name="twrz")
-            for t in range(2):
-                for half in range(2):
-                    nc.tensor.transpose(bank[:, t, half, :],
-                                        words(src[("w", u)][:, t, :])[:, half * P:(half + 1) * P], ident_f[:])
-            tl[("twrz", u)] = bank
+        def transpose_x(u):
+            if absent(u):
+                return
+            made["x_t", u] = psum.tile([P, J, WORDS, P], F32, tag="x_t", name="x_t")
+            transpose_words(made["x_t", u], [x_nat[u][:, j, :] for j in range(J)])
 
-        def s_ewrz(u):
-            nc.scalar.copy(out=words(grouped1(u)[:, 1024:2048]).rearrange("p (a c w) -> p a c w", a=2, c=P, w=2),
-                           in_=tl[("twrz", u)][:].rearrange("p a w c -> p a c w"))
+        def transpose_w_rz(u):
+            if absent(u):
+                return
+            made["w_rz_t", u] = psum.tile([P, 2, WORDS, P], F32, tag="w_rz_t", name="w_rz_t")
+            transpose_words(made["w_rz_t", u], [w_nat[u][:, g, :] for g in range(2)])
 
-        def s_twn(u):
-            bank = ps.tile([P, 2, P], F32, tag="twn", name="twn")
-            for half in range(2):
-                nc.tensor.transpose(bank[:, half, :],
-                                    words(src[("w", u)][:, 2, :])[:, half * P:(half + 1) * P], ident_f[:])
-            tl[("twn", u)] = bank
+        def transpose_w_n(u):
+            if absent(u):
+                return
+            made["w_n_t", u] = psum.tile([P, 1, WORDS, P], F32, tag="w_n_t", name="w_n_t")
+            transpose_words(made["w_n_t", u], [w_nat[u][:, 2, :]])
 
-        def s_ewn(u):
-            g2 = stage.tile([P, 512], BF16, name="g2", align_bytes=64)
-            nc.vector.tensor_copy(out=words(g2[:]).rearrange("p (c w) -> p c w", c=P, w=2),
-                                  in_=tl[("twn", u)][:].rearrange("p w c -> p c w"))
-            tl[("g2", u)] = g2
+        def transpose_hidden(u):
+            if absent(u):
+                return
+            bank = psum.tile([P, J + GATES, P], BF16, tag="hidden_t", name="hidden_t")
+            for j in range(J):
+                nc.tensor.transpose(bank[:, j, :], hidden_rows(u)[:, j, :], ident_b[:])
+            for g in range(GATES):
+                nc.tensor.transpose(bank[:, J + g, :], whh_nat[u][:, g, :], ident_b[:])
+            made["hidden_t", u] = bank
 
-        def s_thh(u):
-            bank = ps.tile([P, 5, P], BF16, tag="thh", name="thh")
-            for j in range(2):
-                nc.tensor.transpose(bank[:, j, :], src[("h", u)][:, j, :], ident_b[:])
-            for t in range(3):
-                nc.tensor.transpose(bank[:, 2 + t, :], src[("g", u)][:, t, :], ident_b[:])
-            tl[("thh", u)] = bank
+        def copy_x(u):
+            if absent(u):
+                return
+            made["x_w_rz", u] = stage.tile([P, (B + 2 * H) * PACK], BF16, name="x_w_rz", align_bytes=64)
+            interleave(nc.scalar.copy, made["x_w_rz", u][:, 0:B * PACK], made["x_t", u])
 
-        def s_ehh(u):
-            hh = const.tile([P, 5, P], BF16, name="hh%d" % u)
-            if u % 2 == 0:
-                nc.scalar.copy(out=hh[:], in_=tl[("thh", u)][:])
-            else:
-                nc.vector.tensor_copy(out=hh[:], in_=tl[("thh", u)][:])
-            tl[("hh", u)] = hh
+        def copy_w_rz(u):
+            if absent(u):
+                return
+            interleave(nc.scalar.copy, made["x_w_rz", u][:, B * PACK:(B + 2 * H) * PACK], made["w_rz_t", u])
 
-        def h_t(u):
-            return tl[("hh", u)][:, 0:2, :].rearrange("p j b -> p (j b)")
+        def copy_w_n(u):
+            if absent(u):
+                return
+            made["w_n", u] = stage.tile([P, H * PACK], BF16, name="w_n", align_bytes=64)
+            interleave(nc.vector.tensor_copy, made["w_n", u][:], made["w_n_t", u])
 
-        def s_q1(u):
-            c = quant.tile([P, 512], U32, name="c1", align_bytes=64)
-            s = quant.tile([P, 512], U8, name="s1", align_bytes=64)
-            nc.vector.quantize_mx(out=c[:].bitcast(FP8X4), scales=s[:], in_=tl[("g1", u)][:])
-            tl[("q1", u)] = (c, s)
+        def copy_hidden(u):
+            if absent(u):
+                return
+            made["hidden", u] = keep.tile([P, J + GATES, P], BF16, name="hidden%d" % u)
+            copy = nc.scalar.copy if u % 2 == 0 else nc.vector.tensor_copy
+            copy(out=made["hidden", u][:], in_=made["hidden_t", u][:])
 
-        def s_q2(u):
-            c = quant.tile([P, P], U32, name="c2", align_bytes=64)
-            s = quant.tile([P, P], U8, name="s2", align_bytes=64)
-            nc.vector.quantize_mx(out=c[:].bitcast(FP8X4), scales=s[:], in_=tl[("g2", u)][:])
-            tl[("q2", u)] = (c, s)
+        def hidden_t(u):
+            return made["hidden", u][:, 0:J, :].rearrange("p j b -> p (j b)")
 
-        def s_apl(u):
-            h1 = ps.tile([P, 512], F32, tag="h1", name="h1")
-            for t in range(2):
-                nc.tensor.matmul(out=h1[:, t * 256:(t + 1) * 256], lhsT=tl[("hh", u)][:, 2 + t, :], rhs=h_t(u),
-                                 start=True, stop=True)
-            tl[("h1", u)] = h1
+        def quantise(u, name):
+            if absent(u):
+                return
+            columns = made[name, u].shape[1] // PACK
+            codes = quant.tile([P, columns], U32, name=name + "_codes", align_bytes=64)
+            scales = quant.tile([P, columns], U8, name=name + "_scales", align_bytes=64)
+            nc.vector.quantize_mx(out=codes[:].bitcast(FP8X4), scales=scales[:], in_=made[name, u][:])
+            made[name + "_q", u] = (codes, scales)
 
-        def s_amx(u):
-            x1 = ps.tile([P, 512], F32, tag="x1", name="x1")
-            c, s = tl[("q1", u)]
-            for t in range(2):
-                ws = slice(256 + t * P, 256 + (t + 1) * P)
-                nc.tensor.matmul_mx(out=x1[:, t * 256:(t + 1) * 256],
-                                    lhsT=c[:, ws].bitcast(FP8X4), lhsT_scale=s[:, ws],
-                                    rhs=c[:, 0:256].bitcast(FP8X4), rhs_scale=s[:, 0:256],
-                                    start=True, stop=True)
-            tl[("x1", u)] = x1
-
-        def s_epl(u):
-            nn = ps.tile([P, 512], F32, tag="nn", name="nn")
-            nc.tensor.matmul(out=nn[:, 0:256], lhsT=tl[("hh", u)][:, 4, :], rhs=h_t(u), start=True, stop=True)
-            tl[("nn", u)] = nn
-
-        def s_emx(u):
-            c, s = tl[("q1", u)]
-            cn, sn = tl[("q2", u)]
-            nc.tensor.matmul_mx(out=tl[("nn", u)][:, 256:512],
-                                lhsT=cn[:].bitcast(FP8X4), lhsT_scale=sn[:],
-                                rhs=c[:, 0:256].bitcast(FP8X4), rhs_scale=s[:, 0:256],
+        def matmul_x(u, acc, weights, first):
+            x_codes, x_scales = made["x_w_rz_q", u]
+            w_codes, w_scales = weights
+            nc.tensor.matmul_mx(out=acc,
+                                lhsT=w_codes[:, first:first + H].bitcast(FP8X4),
+                                lhsT_scale=w_scales[:, first:first + H],
+                                rhs=x_codes[:, 0:B].bitcast(FP8X4), rhs_scale=x_scales[:, 0:B],
                                 start=True, stop=True)
 
-        def s_s1(u):
-            hrz = work.tile([P, 512], F32, name="hrz")
-            nc.scalar.copy(out=hrz[:], in_=tl[("h1", u)][:])
-            tl[("hrz", u)] = hrz
+        def matmul_h(u, acc, g):
+            nc.tensor.matmul(out=acc, lhsT=made["hidden", u][:, J + g, :], rhs=hidden_t(u), start=True, stop=True)
 
-        def s_v1(u):
-            prz = work.tile([P, 512], F32, name="prz")
-            nc.vector.tensor_tensor(out=prz[:], in0=tl[("x1", u)][:], in1=tl[("hrz", u)][:], op=ALU.add)
-            tl[("prz", u)] = prz
+        def matmul_h_rz(u):
+            if absent(u):
+                return
+            made["h_rz", u] = psum.tile([P, 2 * B], F32, tag="h_rz", name="h_rz")
+            for g in range(2):
+                matmul_h(u, made["h_rz", u][:, g * B:(g + 1) * B], g)
 
-        def s_s2(u):
-            r = work.tile([P, 256], F32, name="r")
-            nc.scalar.activation(out=r[:], in_=tl[("prz", u)][:, 0:256], func=ACT.Sigmoid,
-                                 bias=bsum[:, 3 * u:3 * u + 1], scale=1.0)
-            tl[("r", u)] = r
+        def matmul_x_rz(u):
+            if absent(u):
+                return
+            made["x_rz", u] = psum.tile([P, 2 * B], F32, tag="x_rz", name="x_rz")
+            for g in range(2):
+                matmul_x(u, made["x_rz", u][:, g * B:(g + 1) * B], made["x_w_rz_q", u], B + g * H)
 
-        def s_s3(u):
-            zc = work.tile([P, 256], F32, name="zc")
-            nc.scalar.activation(out=zc[:], in_=tl[("prz", u)][:, 256:512], func=ACT.Sigmoid,
-                                 bias=nbsum[:, 3 * u + 1:3 * u + 2], scale=-1.0)
-            tl[("zc", u)] = zc
+        def matmul_n(u):
+            if absent(u):
+                return
+            made["hx_n", u] = psum.tile([P, 2 * B], F32, tag="hx_n", name="hx_n")
+            matmul_h(u, made["hx_n", u][:, 0:B], 2)
+            matmul_x(u, made["hx_n", u][:, B:2 * B], made["w_n_q", u], 0)
 
-        def s_v2(u):
-            m = work.tile([P, 256], F32, name="m")
-            nc.vector.scalar_tensor_tensor(out=m[:], in0=tl[("nn", u)][:, 0:256],
-                                           scalar=bias_cols[:, 48 + 3 * u + 2:48 + 3 * u + 3],
-                                           in1=tl[("r", u)][:], op0=ALU.add, op1=ALU.mult)
-            tl[("m", u)] = m
+        def copy_h_rz(u):
+            if absent(u):
+                return
+            made["h_rz_sb", u] = work.tile([P, 2 * B], F32, name="h_rz_sb")
+            nc.scalar.copy(out=made["h_rz_sb", u][:], in_=made["h_rz", u][:])
 
-        def s_v3(u):
-            v = work.tile([P, 256], F32, name="v")
-            nc.vector.tensor_tensor(out=v[:], in0=tl[("nn", u)][:, 256:512], in1=tl[("m", u)][:], op=ALU.add)
-            tl[("v", u)] = v
+        def add_rz(u):
+            if absent(u):
+                return
+            made["rz", u] = work.tile([P, 2 * B], F32, name="rz")
+            nc.vector.tensor_tensor(out=made["rz", u][:], in0=made["x_rz", u][:], in1=made["h_rz_sb", u][:],
+                                    op=ALU.add)
 
-        def s_s4(u):
-            n = work.tile([P, 256], F32, name="n")
-            nc.scalar.activation(out=n[:], in_=tl[("v", u)][:], func=ACT.Tanh,
-                                 bias=bias_cols[:, 3 * u + 2:3 * u + 3], scale=1.0)
-            tl[("n", u)] = n
+        def reset_gate(u):
+            if absent(u):
+                return
+            made["r", u] = work.tile([P, B], F32, name="r")
+            nc.scalar.activation(out=made["r", u][:], in_=made["rz", u][:, 0:B], func=ACT.Sigmoid,
+                                 bias=column(bias_sum, u * GATES), scale=1.0)
 
-        def blend_engine(u):
-            if False:
-                return nc.vector
-            return nc.gpsimd
+        def update_gate(u):
+            if absent(u):
+                return
+            made["one_minus_z", u] = work.tile([P, B], F32, name="one_minus_z")
+            nc.scalar.activation(out=made["one_minus_z", u][:], in_=made["rz", u][:, B:2 * B], func=ACT.Sigmoid,
+                                 bias=column(bias_neg, u * GATES + 1), scale=-1.0)
 
-        def s_g1(u):
-            d = work.tile([P, 256], F32, name="d")
-            blend_engine(u).tensor_tensor(out=d[:], in0=tl[("n", u)][:], in1=h_t(u), op=ALU.subtract)
-            tl[("d", u)] = d
+        def reset_times_hn(u):
+            if absent(u):
+                return
+            made["r_hn", u] = work.tile([P, B], F32, name="r_hn")
+            nc.vector.scalar_tensor_tensor(out=made["r_hn", u][:], in0=made["hx_n", u][:, 0:B],
+                                           scalar=column(bias_cols, (U + u) * GATES + 2), in1=made["r", u][:],
+                                           op0=ALU.add, op1=ALU.mult)
 
-        def s_g2(u):
-            f = work.tile([P, 256], F32, name="f")
-            blend_engine(u).tensor_tensor(out=f[:], in0=tl[("zc", u)][:], in1=tl[("d", u)][:], op=ALU.mult)
-            tl[("f", u)] = f
+        def add_xn(u):
+            if absent(u):
+                return
+            made["n_sum", u] = work.tile([P, B], F32, name="n_sum")
+            nc.vector.tensor_tensor(out=made["n_sum", u][:], in0=made["hx_n", u][:, B:2 * B],
+                                    in1=made["r_hn", u][:], op=ALU.add)
 
-        def s_tf(u):
-            o_ps = ps.tile([P, 2, P], F32, tag="o", name="o_ps")
-            for j in range(2):
-                nc.tensor.transpose(o_ps[:, j, :], tl[("f", u)][:, j * P:(j + 1) * P], ident_f[:])
-            tl[("o", u)] = o_ps
+        def new_gate(u):
+            if absent(u):
+                return
+            made["n", u] = work.tile([P, B], F32, name="n")
+            nc.scalar.activation(out=made["n", u][:], in_=made["n_sum", u][:], func=ACT.Tanh,
+                                 bias=column(bias_cols, u * GATES + 2), scale=1.0)
 
-        def s_v4(u):
-            q, l = u // 2, u % 2
-            if ("o_sb", q) not in tl:
-                tl[("o_sb", q)] = const.tile([P, 2, 2 * H], F32, name="o_sb%d" % q)
-            nc.vector.tensor_tensor(out=tl[("o_sb", q)][:, :, l * H:(l + 1) * H], in0=tl[("o", u)][:],
-                                    in1=src[("h", u)], op=ALU.add)
+        def blend(u):
+            if absent(u):
+                return
+            engine = nc.gpsimd if u < U - 2 else nc.vector
+            made["n_minus_h", u] = work.tile([P, B], F32, name="n_minus_h")
+            engine.tensor_tensor(out=made["n_minus_h", u][:], in0=made["n", u][:], in1=hidden_t(u), op=ALU.subtract)
+            made["step", u] = work.tile([P, B], F32, name="step")
+            engine.tensor_tensor(out=made["step", u][:], in0=made["one_minus_z", u][:], in1=made["n_minus_h", u][:],
+                                 op=ALU.mult)
 
-        def s_st(u):
+        def transpose_back(u):
+            if absent(u):
+                return
+            made["step_t", u] = psum.tile([P, J, H], F32, tag="step_t", name="step_t")
+            for j in range(J):
+                nc.tensor.transpose(made["step_t", u][:, j, :], made["step", u][:, j * P:(j + 1) * P], ident_f[:])
+
+        def add_hidden_and_store(u):
+            if absent(u):
+                return
+            if u % 2 == 0:
+                made["out", u // 2] = keep.tile([P, J, 2 * H], F32, name="out%d" % (u // 2))
+            pair = made["out", u // 2]
+            nc.vector.tensor_tensor(out=pair[:, :, (u % 2) * H:(u % 2 + 1) * H], in0=made["step_t", u][:],
+                                    in1=hidden_rows(u), op=ALU.add)
             if u % 2 == 1:
-                q = u // 2
-                nc.sync.dma_start(out=out_view[:, :, q * 2 * H:(q + 1) * 2 * H], in_=tl[("o_sb", q)][:])
+                nc.sync.dma_start(out=out_view[:, :, (u - 1) * H:(u + 1) * H], in_=pair[:])
 
-        stages = {"Tx": s_tx, "ex": s_ex, "Twrz": s_twrz, "ewrz": s_ewrz, "Twn": s_twn, "ewn": s_ewn,
-                  "Thh": s_thh, "ehh": s_ehh, "Q1": s_q1, "Q2": s_q2, "Apl": s_apl, "Amx": s_amx,
-                  "Epl": s_epl, "Emx": s_emx, "S1": s_s1, "V1": s_v1, "S2": s_s2, "S3": s_s3,
-                  "V2": s_v2, "V3": s_v3, "S4": s_s4, "G1": s_g1, "G2": s_g2, "Tf": s_tf, "V4": s_v4,
-                  "st": s_st}
+        for i in range(-2, U + 3):
+            copy_x(i + 1)
+            copy_w_rz(i + 1)
+            copy_h_rz(i)
+            reset_gate(i - 1)
+            new_gate(i - 2)
+            copy_w_n(i + 1)
+            copy_hidden(i + 1)
+            update_gate(i - 2)
 
-        for i in range(-3, 22):
-            for name, off in ORDER:
-                u = i + off
-                if 0 <= u < U:
-                    stages[name](u)
+            matmul_n(i - 1)
+            transpose_x(i + 2)
+            transpose_w_rz(i + 2)
+            transpose_back(i - 3)
+
+            quantise(i + 1, "x_w_rz")
+            quantise(i + 1, "w_n")
+            reset_times_hn(i - 1)
+            add_rz(i)
+            add_xn(i - 1)
+            blend(i - 2)
+            add_hidden_and_store(i - 3)
+
+            matmul_h_rz(i + 1)
+            transpose_w_n(i + 2)
+            transpose_hidden(i + 2)
+            matmul_x_rz(i + 1)

@@ -14,6 +14,7 @@ ALU = mybir.AluOpType
 P = 128
 B, U, I, H = 256, 16, 512, 128
 J = B // P
+RESET, UPDATE, NEW = 0, 1, 2
 GATES = 3
 PACK = 4
 WORDS = PACK // 2
@@ -65,7 +66,7 @@ def tile_grouptorchgru_kernel(tc, inputs, hidden, w_ih, w_hh, b_ih, b_hh, out):
         def hidden_rows(u):
             return h_nat[u // QUAD][:, :, (u % QUAD) * H:(u % QUAD + 1) * H]
 
-        bias_ps = psum.tile([P, J + GATES, P], BF16, tag="hidden_t", name="bias_ps")
+        bias_ps = psum.tile([P, J + GATES, P], BF16, tag="h_side_t", name="bias_ps")
         nc.tensor.transpose(bias_ps[:, 0, :], bias_rows[:], ident_b[:])
         bias_cols = keep.tile([P, P], F32, name="bias_cols")
         nc.vector.tensor_copy(out=bias_cols[:], in_=bias_ps[:, 0, :])
@@ -102,23 +103,23 @@ def tile_grouptorchgru_kernel(tc, inputs, hidden, w_ih, w_hh, b_ih, b_hh, out):
             if absent(u):
                 return
             made["w_rz_t", u] = psum.tile([P, 2, WORDS, P], F32, tag="w_rz_t", name="w_rz_t")
-            transpose_words(made["w_rz_t", u], [w_nat[u][:, g, :] for g in range(2)])
+            transpose_words(made["w_rz_t", u], [w_nat[u][:, g, :] for g in (RESET, UPDATE)])
 
         def transpose_w_n(u):
             if absent(u):
                 return
             made["w_n_t", u] = psum.tile([P, 1, WORDS, P], F32, tag="w_n_t", name="w_n_t")
-            transpose_words(made["w_n_t", u], [w_nat[u][:, 2, :]])
+            transpose_words(made["w_n_t", u], [w_nat[u][:, NEW, :]])
 
-        def transpose_hidden(u):
+        def transpose_h_side(u):
             if absent(u):
                 return
-            bank = psum.tile([P, J + GATES, P], BF16, tag="hidden_t", name="hidden_t")
+            bank = psum.tile([P, J + GATES, P], BF16, tag="h_side_t", name="h_side_t")
             for j in range(J):
                 nc.tensor.transpose(bank[:, j, :], hidden_rows(u)[:, j, :], ident_b[:])
             for g in range(GATES):
                 nc.tensor.transpose(bank[:, J + g, :], whh_nat[u][:, g, :], ident_b[:])
-            made["hidden_t", u] = bank
+            made["h_side_t", u] = bank
 
         def copy_x(u):
             if absent(u):
@@ -137,15 +138,15 @@ def tile_grouptorchgru_kernel(tc, inputs, hidden, w_ih, w_hh, b_ih, b_hh, out):
             made["w_n", u] = stage.tile([P, H * PACK], BF16, name="w_n", align_bytes=64)
             interleave(nc.vector.tensor_copy, made["w_n", u][:], made["w_n_t", u])
 
-        def copy_hidden(u):
+        def copy_h_side(u):
             if absent(u):
                 return
-            made["hidden", u] = keep.tile([P, J + GATES, P], BF16, name="hidden%d" % u)
+            made["h_side", u] = keep.tile([P, J + GATES, P], BF16, name="h_side%d" % u)
             copy = nc.scalar.copy if u % 2 == 0 else nc.vector.tensor_copy
-            copy(out=made["hidden", u][:], in_=made["hidden_t", u][:])
+            copy(out=made["h_side", u][:], in_=made["h_side_t", u][:])
 
         def hidden_t(u):
-            return made["hidden", u][:, 0:J, :].rearrange("p j b -> p (j b)")
+            return made["h_side", u][:, 0:J, :].rearrange("p j b -> p (j b)")
 
         def quantise(u, name):
             if absent(u):
@@ -166,27 +167,27 @@ def tile_grouptorchgru_kernel(tc, inputs, hidden, w_ih, w_hh, b_ih, b_hh, out):
                                 start=True, stop=True)
 
         def matmul_h(u, acc, g):
-            nc.tensor.matmul(out=acc, lhsT=made["hidden", u][:, J + g, :], rhs=hidden_t(u), start=True, stop=True)
+            nc.tensor.matmul(out=acc, lhsT=made["h_side", u][:, J + g, :], rhs=hidden_t(u), start=True, stop=True)
 
         def matmul_h_rz(u):
             if absent(u):
                 return
             made["h_rz", u] = psum.tile([P, 2 * B], F32, tag="h_rz", name="h_rz")
-            for g in range(2):
+            for g in (RESET, UPDATE):
                 matmul_h(u, made["h_rz", u][:, g * B:(g + 1) * B], g)
 
         def matmul_x_rz(u):
             if absent(u):
                 return
             made["x_rz", u] = psum.tile([P, 2 * B], F32, tag="x_rz", name="x_rz")
-            for g in range(2):
+            for g in (RESET, UPDATE):
                 matmul_x(u, made["x_rz", u][:, g * B:(g + 1) * B], made["x_w_rz_q", u], B + g * H)
 
         def matmul_n(u):
             if absent(u):
                 return
             made["hx_n", u] = psum.tile([P, 2 * B], F32, tag="hx_n", name="hx_n")
-            matmul_h(u, made["hx_n", u][:, 0:B], 2)
+            matmul_h(u, made["hx_n", u][:, 0:B], NEW)
             matmul_x(u, made["hx_n", u][:, B:2 * B], made["w_n_q", u], 0)
 
         def copy_h_rz(u):
@@ -207,21 +208,21 @@ def tile_grouptorchgru_kernel(tc, inputs, hidden, w_ih, w_hh, b_ih, b_hh, out):
                 return
             made["r", u] = work.tile([P, B], F32, name="r")
             nc.scalar.activation(out=made["r", u][:], in_=made["rz", u][:, 0:B], func=ACT.Sigmoid,
-                                 bias=column(bias_sum, u * GATES), scale=1.0)
+                                 bias=column(bias_sum, u * GATES + RESET), scale=1.0)
 
         def update_gate(u):
             if absent(u):
                 return
             made["one_minus_z", u] = work.tile([P, B], F32, name="one_minus_z")
             nc.scalar.activation(out=made["one_minus_z", u][:], in_=made["rz", u][:, B:2 * B], func=ACT.Sigmoid,
-                                 bias=column(bias_neg, u * GATES + 1), scale=-1.0)
+                                 bias=column(bias_neg, u * GATES + UPDATE), scale=-1.0)
 
         def reset_times_hn(u):
             if absent(u):
                 return
             made["r_hn", u] = work.tile([P, B], F32, name="r_hn")
             nc.vector.scalar_tensor_tensor(out=made["r_hn", u][:], in0=made["hx_n", u][:, 0:B],
-                                           scalar=column(bias_cols, (U + u) * GATES + 2), in1=made["r", u][:],
+                                           scalar=column(bias_cols, (U + u) * GATES + NEW), in1=made["r", u][:],
                                            op0=ALU.add, op1=ALU.mult)
 
         def add_xn(u):
@@ -236,7 +237,7 @@ def tile_grouptorchgru_kernel(tc, inputs, hidden, w_ih, w_hh, b_ih, b_hh, out):
                 return
             made["n", u] = work.tile([P, B], F32, name="n")
             nc.scalar.activation(out=made["n", u][:], in_=made["n_sum", u][:], func=ACT.Tanh,
-                                 bias=column(bias_cols, u * GATES + 2), scale=1.0)
+                                 bias=column(bias_cols, u * GATES + NEW), scale=1.0)
 
         def blend(u):
             if absent(u):
@@ -273,7 +274,7 @@ def tile_grouptorchgru_kernel(tc, inputs, hidden, w_ih, w_hh, b_ih, b_hh, out):
             reset_gate(i - 1)
             new_gate(i - 2)
             copy_w_n(i + 1)
-            copy_hidden(i + 1)
+            copy_h_side(i + 1)
             update_gate(i - 2)
 
             matmul_n(i - 1)
@@ -291,5 +292,5 @@ def tile_grouptorchgru_kernel(tc, inputs, hidden, w_ih, w_hh, b_ih, b_hh, out):
 
             matmul_h_rz(i + 1)
             transpose_w_n(i + 2)
-            transpose_hidden(i + 2)
+            transpose_h_side(i + 2)
             matmul_x_rz(i + 1)

from contextlib import ExitStack

import concourse.masks as masks
import concourse.mybir as mybir

F32 = mybir.dt.float32
BF16 = mybir.dt.bfloat16
U32 = mybir.dt.uint32
U8 = mybir.dt.uint8
FP8X4 = mybir.dt.float8_e4m3fn_x4
ACT = mybir.ActivationFunctionType
ALU = mybir.AluOpType

P = 128
B, U, I, H = 256, 16, 512, 128
J = B // P
RESET, UPDATE, NEW = 0, 1, 2
GATES = 3
PACK = 4
WORDS = PACK // 2
QUAD = 4
FLOPS = 2 * B * U * GATES * H * (I + H)


def tile_grouptorchgru_kernel(tc, inputs, hidden, w_ih, w_hh, b_ih, b_hh, out):
    nc = tc.nc
    x_view = inputs.rearrange("(j p) u k -> p j (u k)", p=P)
    h_view = hidden.rearrange("(j p) u h -> p j (u h)", p=P)
    out_view = out.rearrange("(j p) u h -> p j (u h)", p=P)
    w_view = w_ih.flatten_outer_dims().rearrange("(g p) k -> p g k", p=P)
    whh_view = w_hh.flatten_outer_dims().rearrange("(g p) k -> p g k", p=P)

    with ExitStack() as ctx:
        keep = ctx.enter_context(tc.tile_pool(name="keep", bufs=1))
        stage = ctx.enter_context(tc.tile_pool(name="stage", bufs=2))
        quant = ctx.enter_context(tc.tile_pool(name="quant", bufs=3))
        work = ctx.enter_context(tc.tile_pool(name="work", bufs=3))
        psum = ctx.enter_context(tc.psum_pool(name="psum", bufs=1))
        ctx.enter_context(tc.manual_schedule())

        bias_rows = keep.tile([P, P], BF16, name="bias_rows")
        nc.scalar.dma_start(out=bias_rows[0:U * GATES, :], in_=b_ih.rearrange("u (g h) -> (u g) h", h=H))
        nc.scalar.dma_start(out=bias_rows[U * GATES:2 * U * GATES, :],
                            in_=b_hh.rearrange("u (g h) -> (u g) h", h=H))
        nc.vector.memset(bias_rows[2 * U * GATES:P, :], 0.0)
        warm = keep.tile([P, 2], F32, name="warm")
        nc.vector.memset(warm[:], 0.0)
        nc.scalar.activation(out=warm[:, 1:2], in_=warm[:, 0:1], func=ACT.Sigmoid)
        ident_b = keep.tile([P, P], BF16, name="ident_b")
        masks.make_identity(nc, ident_b[:])
        ident_f = keep.tile([P, P], F32, name="ident_f")
        masks.make_identity(nc, ident_f[:])

        x_nat, w_nat, whh_nat, h_nat = [], [], [], []
        for u in range(U):
            x_nat.append(keep.tile([P, J, I], BF16, name="x_nat%d" % u))
            nc.sync.dma_start(out=x_nat[u][:], in_=x_view[:, :, u * I:(u + 1) * I])
            w_nat.append(keep.tile([P, GATES, I], BF16, name="w_nat%d" % u))
            nc.sync.dma_start(out=w_nat[u][:], in_=w_view[:, u * GATES:(u + 1) * GATES, :])
            if u % QUAD == 0:
                h_nat.append(keep.tile([P, J, QUAD * H], BF16, name="h_nat%d" % (u // QUAD)))
                nc.sync.dma_start(out=h_nat[u // QUAD][:], in_=h_view[:, :, u * H:(u + QUAD) * H])
            whh_nat.append(keep.tile([P, GATES, H], BF16, name="whh_nat%d" % u))
            nc.sync.dma_start(out=whh_nat[u][:], in_=whh_view[:, u * GATES:(u + 1) * GATES, :])

        def hidden_rows(u):
            return h_nat[u // QUAD][:, :, (u % QUAD) * H:(u % QUAD + 1) * H]

        bias_ps = psum.tile([P, J + GATES, P], BF16, tag="h_side_t", name="bias_ps")
        nc.tensor.transpose(bias_ps[:, 0, :], bias_rows[:], ident_b[:])
        bias_cols = keep.tile([P, P], F32, name="bias_cols")
        nc.vector.tensor_copy(out=bias_cols[:], in_=bias_ps[:, 0, :])
        bias_sum = keep.tile([P, U * GATES], F32, name="bias_sum")
        nc.vector.tensor_tensor(out=bias_sum[:], in0=bias_cols[:, 0:U * GATES],
                                in1=bias_cols[:, U * GATES:2 * U * GATES], op=ALU.add)
        bias_neg = keep.tile([P, U * GATES], F32, name="bias_neg")
        nc.vector.tensor_scalar_mul(out=bias_neg[:], in0=bias_sum[:], scalar1=-1.0)

        def column(table, index):
            return table[:, index:index + 1]

        made = {}

        def absent(u):
            return u < 0 or u >= U

        def transpose_words(bank, rows):
            for a in range(len(rows)):
                for w in range(WORDS):
                    nc.tensor.transpose(bank[:, a, w, :], rows[a].bitcast(F32)[:, w * P:(w + 1) * P], ident_f[:])

        def interleave(copy, grouped, bank):
            copy(out=grouped.bitcast(F32).rearrange("p (a c w) -> p a c w", c=P, w=WORDS),
                 in_=bank[:].rearrange("p a w c -> p a c w"))

        def transpose_x(u):
            if absent(u):
                return
            made["x_t", u] = psum.tile([P, J, WORDS, P], F32, tag="x_t", name="x_t")
            transpose_words(made["x_t", u], [x_nat[u][:, j, :] for j in range(J)])

        def transpose_w_rz(u):
            if absent(u):
                return
            made["w_rz_t", u] = psum.tile([P, 2, WORDS, P], F32, tag="w_rz_t", name="w_rz_t")
            transpose_words(made["w_rz_t", u], [w_nat[u][:, g, :] for g in (RESET, UPDATE)])

        def transpose_w_n(u):
            if absent(u):
                return
            made["w_n_t", u] = psum.tile([P, 1, WORDS, P], F32, tag="w_n_t", name="w_n_t")
            transpose_words(made["w_n_t", u], [w_nat[u][:, NEW, :]])

        def transpose_h_side(u):
            if absent(u):
                return
            bank = psum.tile([P, J + GATES, P], BF16, tag="h_side_t", name="h_side_t")
            for j in range(J):
                nc.tensor.transpose(bank[:, j, :], hidden_rows(u)[:, j, :], ident_b[:])
            for g in range(GATES):
                nc.tensor.transpose(bank[:, J + g, :], whh_nat[u][:, g, :], ident_b[:])
            made["h_side_t", u] = bank

        def copy_x(u):
            if absent(u):
                return
            made["x_w_rz", u] = stage.tile([P, (B + 2 * H) * PACK], BF16, name="x_w_rz", align_bytes=64)
            interleave(nc.scalar.copy, made["x_w_rz", u][:, 0:B * PACK], made["x_t", u])

        def copy_w_rz(u):
            if absent(u):
                return
            interleave(nc.scalar.copy, made["x_w_rz", u][:, B * PACK:(B + 2 * H) * PACK], made["w_rz_t", u])

        def copy_w_n(u):
            if absent(u):
                return
            made["w_n", u] = stage.tile([P, H * PACK], BF16, name="w_n", align_bytes=64)
            interleave(nc.vector.tensor_copy, made["w_n", u][:], made["w_n_t", u])

        def copy_h_side(u):
            if absent(u):
                return
            made["h_side", u] = keep.tile([P, J + GATES, P], BF16, name="h_side%d" % u)
            copy = nc.scalar.copy if u % 2 == 0 else nc.vector.tensor_copy
            copy(out=made["h_side", u][:], in_=made["h_side_t", u][:])

        def hidden_t(u):
            return made["h_side", u][:, 0:J, :].rearrange("p j b -> p (j b)")

        def quantise(u, name):
            if absent(u):
                return
            columns = made[name, u].shape[1] // PACK
            codes = quant.tile([P, columns], U32, name=name + "_codes", align_bytes=64)
            scales = quant.tile([P, columns], U8, name=name + "_scales", align_bytes=64)
            nc.vector.quantize_mx(out=codes[:].bitcast(FP8X4), scales=scales[:], in_=made[name, u][:])
            made[name + "_q", u] = (codes, scales)

        def matmul_x(u, acc, weights, first):
            x_codes, x_scales = made["x_w_rz_q", u]
            w_codes, w_scales = weights
            nc.tensor.matmul_mx(out=acc,
                                lhsT=w_codes[:, first:first + H].bitcast(FP8X4),
                                lhsT_scale=w_scales[:, first:first + H],
                                rhs=x_codes[:, 0:B].bitcast(FP8X4), rhs_scale=x_scales[:, 0:B],
                                start=True, stop=True)

        def matmul_h(u, acc, g):
            nc.tensor.matmul(out=acc, lhsT=made["h_side", u][:, J + g, :], rhs=hidden_t(u), start=True, stop=True)

        def matmul_h_rz(u):
            if absent(u):
                return
            made["h_rz", u] = psum.tile([P, 2 * B], F32, tag="h_rz", name="h_rz")
            for g in (RESET, UPDATE):
                matmul_h(u, made["h_rz", u][:, g * B:(g + 1) * B], g)

        def matmul_x_rz(u):
            if absent(u):
                return
            made["x_rz", u] = psum.tile([P, 2 * B], F32, tag="x_rz", name="x_rz")
            for g in (RESET, UPDATE):
                matmul_x(u, made["x_rz", u][:, g * B:(g + 1) * B], made["x_w_rz_q", u], B + g * H)

        def matmul_n(u):
            if absent(u):
                return
            made["hx_n", u] = psum.tile([P, 2 * B], F32, tag="hx_n", name="hx_n")
            matmul_h(u, made["hx_n", u][:, 0:B], NEW)
            matmul_x(u, made["hx_n", u][:, B:2 * B], made["w_n_q", u], 0)

        def copy_h_rz(u):
            if absent(u):
                return
            made["h_rz_sb", u] = work.tile([P, 2 * B], F32, name="h_rz_sb")
            nc.scalar.copy(out=made["h_rz_sb", u][:], in_=made["h_rz", u][:])

        def add_rz(u):
            if absent(u):
                return
            made["rz", u] = work.tile([P, 2 * B], F32, name="rz")
            nc.vector.tensor_tensor(out=made["rz", u][:], in0=made["x_rz", u][:], in1=made["h_rz_sb", u][:],
                                    op=ALU.add)

        def reset_gate(u):
            if absent(u):
                return
            made["r", u] = work.tile([P, B], F32, name="r")
            nc.scalar.activation(out=made["r", u][:], in_=made["rz", u][:, 0:B], func=ACT.Sigmoid,
                                 bias=column(bias_sum, u * GATES + RESET), scale=1.0)

        def update_gate(u):
            if absent(u):
                return
            made["one_minus_z", u] = work.tile([P, B], F32, name="one_minus_z")
            nc.scalar.activation(out=made["one_minus_z", u][:], in_=made["rz", u][:, B:2 * B], func=ACT.Sigmoid,
                                 bias=column(bias_neg, u * GATES + UPDATE), scale=-1.0)

        def reset_times_hn(u):
            if absent(u):
                return
            made["r_hn", u] = work.tile([P, B], F32, name="r_hn")
            nc.vector.scalar_tensor_tensor(out=made["r_hn", u][:], in0=made["hx_n", u][:, 0:B],
                                           scalar=column(bias_cols, (U + u) * GATES + NEW), in1=made["r", u][:],
                                           op0=ALU.add, op1=ALU.mult)

        def add_xn(u):
            if absent(u):
                return
            made["n_sum", u] = work.tile([P, B], F32, name="n_sum")
            nc.vector.tensor_tensor(out=made["n_sum", u][:], in0=made["hx_n", u][:, B:2 * B],
                                    in1=made["r_hn", u][:], op=ALU.add)

        def new_gate(u):
            if absent(u):
                return
            made["n", u] = work.tile([P, B], F32, name="n")
            nc.scalar.activation(out=made["n", u][:], in_=made["n_sum", u][:], func=ACT.Tanh,
                                 bias=column(bias_cols, u * GATES + NEW), scale=1.0)

        def blend(u):
            if absent(u):
                return
            engine = nc.gpsimd if u < U - 2 else nc.vector
            made["n_minus_h", u] = work.tile([P, B], F32, name="n_minus_h")
            engine.tensor_tensor(out=made["n_minus_h", u][:], in0=made["n", u][:], in1=hidden_t(u), op=ALU.subtract)
            made["step", u] = work.tile([P, B], F32, name="step")
            engine.tensor_tensor(out=made["step", u][:], in0=made["one_minus_z", u][:], in1=made["n_minus_h", u][:],
                                 op=ALU.mult)

        def transpose_back(u):
            if absent(u):
                return
            made["step_t", u] = psum.tile([P, J, H], F32, tag="step_t", name="step_t")
            for j in range(J):
                nc.tensor.transpose(made["step_t", u][:, j, :], made["step", u][:, j * P:(j + 1) * P], ident_f[:])

        def add_hidden_and_store(u):
            if absent(u):
                return
            if u % 2 == 0:
                made["out", u // 2] = keep.tile([P, J, 2 * H], F32, name="out%d" % (u // 2))
            pair = made["out", u // 2]
            nc.vector.tensor_tensor(out=pair[:, :, (u % 2) * H:(u % 2 + 1) * H], in0=made["step_t", u][:],
                                    in1=hidden_rows(u), op=ALU.add)
            if u % 2 == 1:
                nc.sync.dma_start(out=out_view[:, :, (u - 1) * H:(u + 1) * H], in_=pair[:])

        for i in range(-2, U + 3):
            copy_x(i + 1)
            copy_w_rz(i + 1)
            copy_h_rz(i)
            reset_gate(i - 1)
            new_gate(i - 2)
            copy_w_n(i + 1)
            copy_h_side(i + 1)
            update_gate(i - 2)

            matmul_n(i - 1)
            transpose_x(i + 2)
            transpose_w_rz(i + 2)
            transpose_back(i - 3)

            quantise(i + 1, "x_w_rz")
            quantise(i + 1, "w_n")
            reset_times_hn(i - 1)
            add_rz(i)
            add_xn(i - 1)
            blend(i - 2)
            add_hidden_and_store(i - 3)

            matmul_h_rz(i + 1)
            transpose_w_n(i + 2)
            transpose_h_side(i + 2)
            matmul_x_rz(i + 1)
